import numpy as np
import ml_dtypes


def mxq(x, axis, fmt="e4m3"):
    dtype, down = {"e4m3": (ml_dtypes.float8_e4m3fn, 7), "e5m2": (ml_dtypes.float8_e5m2, 14)}[fmt]
    v = np.moveaxis(np.asarray(x, np.float32).astype(ml_dtypes.bfloat16).astype(np.float64), axis, -1)
    blocks = v.reshape(v.shape[:-1] + (-1, 32))
    amax = np.abs(blocks).max(-1, keepdims=True)
    byte = np.maximum(np.where(amax > 0, np.frexp(amax)[1] - 1 + 127, 0) - down, 1)
    scale = np.exp2(byte - 127.0)
    codes = (blocks / scale).astype(np.float32).astype(dtype).astype(np.float64)
    return np.moveaxis((codes * scale).reshape(v.shape), -1, axis)


WIDE = False


def mx_kscale(k):
    if not WIDE:
        return np.ones(k)
    levels = np.array([10, -10, 5, -5, 0])
    a = np.random.permutation(np.resize(levels, k // 512 * 4)).reshape(k // 512, 4)
    idx = np.arange(k)
    return np.exp2(a[idx // 512, idx % 128 // 32])


BF16 = ml_dtypes.bfloat16


def bf(x):
    return np.asarray(x, np.float32).astype(BF16)


def f64(x):
    return np.asarray(x).astype(np.float64)


B, S, D, QC, KVC, FF = 2, 2048, 1024, 16, 2, 4096
HD = D // QC
REP = QC // KVC
KV = KVC * HD
EPS = 1e-5


def rotate_every_two(u):
    u1 = u[..., ::2]
    u2 = u[..., 1::2]
    return np.stack((-u2, u1), axis=-1).reshape(*u.shape[:-1], -1)


def apply_rope(u, sin, cos):
    return u * cos + rotate_every_two(u) * sin


def rmsnorm(u, w):
    return u / np.sqrt(np.square(u).mean(-1, keepdims=True) + EPS) * w


def setup_inputs():
    s = mx_kscale(D)
    pos = np.arange(S, dtype=np.float64)
    inv_freq = 1.0 / (10000.0 ** (np.arange(0, HD, 2, dtype=np.float64) / HD))
    freqs = pos[:, None] * inv_freq[None, :]
    return {"x": bf(np.random.standard_normal((B, S, D))),
            "norm1_w": bf((1.0 + 0.1 * np.random.standard_normal(D)) * s),
            "wqkv": bf(np.random.standard_normal((D, D + 2 * KV)) * 1.5 / np.sqrt(D) / s[:, None]),
            "rope_sin": bf(np.repeat(np.sin(freqs), 2, axis=-1)),
            "rope_cos": bf(np.repeat(np.cos(freqs), 2, axis=-1))}


def reference(x, norm1_w, wqkv, rope_sin, rope_cos):
    sin = f64(rope_sin)[:S]
    cos = f64(rope_cos)[:S]
    xn = rmsnorm(f64(x), f64(norm1_w))
    qkv = mxq(xn, 2, "e4m3") @ mxq(f64(wqkv), 0, "e4m3")
    q = np.moveaxis(qkv[..., :D].reshape(B, S, REP, KVC, HD), 1, 3)
    q = apply_rope(q, sin, cos)
    k, v = np.split(qkv[..., D:], 2, axis=-1)
    k = k.reshape(B, S, KVC, HD).swapaxes(1, 2)
    v = v.reshape(B, S, KVC, HD).swapaxes(1, 2)
    k = apply_rope(k, sin, cos) * HD ** -0.5
    return q, k, v

@@ -1,0 +1,252 @@
+from contextlib import ExitStack
+
+import concourse.mybir as mybir
+from concourse.masks import make_identity
+
+F32 = mybir.dt.float32
+BF16 = mybir.dt.bfloat16
+U32 = mybir.dt.uint32
+U8 = mybir.dt.uint8
+FP8X4 = mybir.dt.float8_e4m3fn_x4
+ALU = mybir.AluOpType
+ACT = mybir.ActivationFunctionType
+
+P = 128
+BATCH = 2
+SEQ = 2048
+D = 1024
+HD = 64
+HALF = HD // 2
+Q_HEADS = 16
+KV_HEADS = 2
+ROPED_HEADS = Q_HEADS + KV_HEADS
+HEADS = Q_HEADS + 2 * KV_HEADS
+N_OUT = HEADS * HD
+EPS = 1e-5
+
+PACK = 4
+K_PASS = P * PACK
+PASSES = D // K_PASS
+K_BLOCKS = D // P
+
+TOK = SEQ // P
+CHUNK = 4
+TILES = BATCH * TOK
+CHUNKS = TILES // CHUNK
+BANK = 512
+BANK_HEADS = BANK // HD
+
+FLOPS = 2 * BATCH * SEQ * D * N_OUT
+
+
+def tile_block_pa_t_kernel(
+    tc, x, norm1_w, wqkv, rope_sin, rope_cos, out_0, out_1, out_2
+):
+    nc = tc.nc
+
+    x_view = x.rearrange("b (p t) k -> b p t k", t=TOK)
+    q_view = out_0.rearrange("b r g (p t) d -> b p (r g) t d", t=TOK)
+    k_view = out_1.rearrange("b g (p t) d -> b p g t d", t=TOK)
+    v_view = out_2.rearrange("b g (p t) d -> b p g t d", t=TOK)
+
+    with ExitStack() as ctx:
+        const = ctx.enter_context(tc.tile_pool(name="const", bufs=1))
+        x_pool = ctx.enter_context(tc.tile_pool(name="x_pool", bufs=4))
+        stat = ctx.enter_context(tc.tile_pool(name="stat", bufs=3))
+        work = ctx.enter_context(tc.tile_pool(name="work", bufs=3))
+        out_pool = ctx.enter_context(tc.tile_pool(name="out_pool", bufs=3))
+        xt_psum = ctx.enter_context(tc.psum_pool(name="xt_psum", bufs=2))
+        acc_psum = ctx.enter_context(tc.psum_pool(name="acc_psum", bufs=2))
+
+        x_tiles = {}
+        rstd_tiles = {}
+        grouped_tiles = {}
+        acc_tiles = {}
+        out_tiles = {}
+
+        def load_x(chunk):
+            b, t0 = divmod(chunk * CHUNK, TOK)
+            x_sb = x_pool.tile([P, CHUNK, D], BF16)
+            nc.sync.dma_start(out=x_sb[:], in_=x_view[b, :, t0 : t0 + CHUNK, :])
+            x_tiles[chunk] = x_sb
+
+        load_x(0)
+        gain = const.tile([P, D], BF16)
+        nc.scalar.dma_start(out=gain[:], in_=norm1_w.partition_broadcast(P))
+        w_raw = const.tile([P, K_BLOCKS, N_OUT], BF16)
+        w_rows = wqkv.rearrange("(kb p) n -> p kb n", p=P)
+        for c in range(PASSES):
+            slots = slice(c * PACK, (c + 1) * PACK)
+            nc.sync.dma_start(out=w_raw[:, slots, :], in_=w_rows[:, slots, :])
+        cos_raw = const.tile([P, TOK, HD], BF16)
+        nc.sync.dma_start(out=cos_raw[:], in_=rope_cos.rearrange("(p t) d -> p t d", t=TOK))
+        sin_raw = const.tile([P, TOK, HD], BF16)
+        nc.sync.dma_start(out=sin_raw[:], in_=rope_sin.rearrange("(p t) d -> p t d", t=TOK))
+        for chunk in range(1, 4):
+            load_x(chunk)
+
+        eps = const.tile([P, 1], F32)
+        nc.vector.memset(eps[:], EPS)
+        warm = const.tile([P, 1], F32)
+        nc.scalar.activation(out=warm[:], in_=eps[:], func=ACT.Sqrt)
+        ident = const.tile([P, P], BF16)
+        make_identity(nc, ident[:])
+
+        sin_pairs = sin_raw[:].rearrange("p t (i e) -> p t e i", e=2)
+        sin_q = const.tile([P, TOK, 2, HALF], F32)
+        sin_k = const.tile([P, TOK, 2, HALF], F32)
+        cos_k = const.tile([P, TOK, HD], F32)
+        k_scale = HD**-0.5
+        for table, scale in ((sin_q, 1.0), (sin_k, k_scale)):
+            for e, sign in ((0, -1.0), (1, 1.0)):
+                nc.gpsimd.tensor_scalar(
+                    out=table[:, :, e, :],
+                    in0=sin_pairs[:, :, e, :],
+                    scalar1=sign * scale,
+                    scalar2=0.0,
+                    op0=ALU.mult,
+                    op1=ALU.add,
+                )
+        nc.gpsimd.tensor_scalar(
+            out=cos_k[:], in0=cos_raw[:], scalar1=k_scale, scalar2=0.0, op0=ALU.mult, op1=ALU.add
+        )
+
+        w_grouped = const.tile([P, PASSES, N_OUT, PACK], BF16, align_bytes=64)
+        w_codes = const.tile([P, PASSES, N_OUT], U32, align_bytes=64)
+        w_scales = const.tile([P, PASSES, N_OUT], U8, align_bytes=64)
+        for c in range(PASSES):
+            src = w_raw[:, c * PACK : (c + 1) * PACK, :].rearrange("p j (m i) -> p m j i", i=4)
+            dst = w_grouped[:, c, :, :].rearrange("p (m i) j -> p m j i", i=4)
+            if c == 0:
+                nc.vector.tensor_copy(out=dst, in_=src)
+            else:
+                nc.scalar.copy(out=dst, in_=src)
+        for c in range(PASSES):
+            for n0, n1 in ((0, 1024), (1024, N_OUT)):
+                nc.vector.quantize_mx(
+                    out=w_codes[:, c, n0:n1].bitcast(FP8X4),
+                    scales=w_scales[:, c, n0:n1],
+                    in_=w_grouped[:, c, n0:n1, :].rearrange("p n j -> p (n j)"),
+                )
+
+        def statistics(chunk):
+            x_sb = x_tiles[chunk]
+            sum_sq = stat.tile([P, CHUNK], F32)
+            for j in range(CHUNK):
+                squares = work.tile([P, D], BF16)
+                nc.scalar.activation(
+                    out=squares[:], in_=x_sb[:, j, :], func=ACT.Square,
+                    accum_out=sum_sq[:, j : j + 1],
+                )
+            rms = stat.tile([P, CHUNK], F32)
+            nc.scalar.activation(out=rms[:], in_=sum_sq[:], func=ACT.Sqrt, bias=eps[:], scale=1.0 / D)
+            rstd = stat.tile([P, CHUNK], F32)
+            nc.vector.reciprocal(out=rstd[:], in_=rms[:])
+            rstd_tiles[chunk] = rstd
+
+        def normalise_and_transpose(n):
+            chunk, j = divmod(n, CHUNK)
+            xn = work.tile([P, D], BF16)
+            nc.vector.scalar_tensor_tensor(
+                out=xn[:], in0=x_tiles[chunk][:, j, :], scalar=rstd_tiles[chunk][:, j : j + 1],
+                in1=gain[:], op0=ALU.mult, op1=ALU.mult,
+            )
+            xt = xt_psum.tile([P, K_BLOCKS, P], BF16)
+            for kb in range(K_BLOCKS):
+                nc.tensor.transpose(xt[:, kb, :], xn[:, kb * P : (kb + 1) * P], ident[:])
+            grouped = work.tile([P, PASSES, P, PACK], BF16, align_bytes=64)
+            nc.scalar.copy(out=grouped[:], in_=xt[:].rearrange("p (c j) r -> p c r j", j=PACK))
+            grouped_tiles[n] = grouped
+
+        def quantise_and_multiply(n):
+            codes = work.tile([P, PASSES, P], U32, align_bytes=64)
+            scales = work.tile([P, PASSES, P], U8, align_bytes=64)
+            nc.vector.quantize_mx(
+                out=codes[:].rearrange("p c r -> p (c r)").bitcast(FP8X4),
+                scales=scales[:].rearrange("p c r -> p (c r)"),
+                in_=grouped_tiles.pop(n)[:].rearrange("p c r j -> p (c r j)"),
+            )
+            acc_q0 = acc_psum.tile([P, BANK], F32)
+            acc_q1 = acc_psum.tile([P, BANK], F32)
+            acc_kv = acc_psum.tile([P, 2 * KV_HEADS * HD], F32)
+            n0 = 0
+            for acc in (acc_q0, acc_q1, acc_kv):
+                width = acc.shape[1]
+                for c in range(PASSES):
+                    nc.tensor.matmul_mx(
+                        out=acc[:],
+                        lhsT=codes[:, c, :].bitcast(FP8X4),
+                        lhsT_scale=scales[:, c, :],
+                        rhs=w_codes[:, c, n0 : n0 + width].bitcast(FP8X4),
+                        rhs_scale=w_scales[:, c, n0 : n0 + width],
+                        start=(c == 0),
+                        stop=(c == PASSES - 1),
+                    )
+                n0 += width
+            acc_tiles[n] = (acc_q0, acc_q1, acc_kv)
+
+        def rope_products(u, heads, cos_row, sin_rows, straight, cross):
+            nc.vector.tensor_tensor(
+                out=straight,
+                in0=u.rearrange("p (h d) -> p h d", d=HD),
+                in1=cos_row.unsqueeze(1).to_broadcast([P, heads, HD]),
+                op=ALU.mult,
+            )
+            pairs = u.rearrange("p (h i e) -> p h i e", i=HALF, e=2)
+            for e in range(2):
+                nc.vector.tensor_tensor(
+                    out=cross[:, e, :, :],
+                    in0=pairs[:, :, :, 1 - e],
+                    in1=sin_rows[:, e, :].unsqueeze(1).to_broadcast([P, heads, HALF]),
+                    op=ALU.mult,
+                )
+
+        def rope_and_store(n):
+            chunk, j = divmod(n, CHUNK)
+            b, t0 = divmod(chunk * CHUNK, TOK)
+            t = t0 + j
+            if j == 0:
+                out_sb = out_pool.tile([P, HEADS, CHUNK, HD], F32)
+                out_tiles[chunk] = out_sb
+            out_sb = out_tiles[chunk]
+            acc_q0, acc_q1, acc_kv = acc_tiles.pop(n)
+            cross = work.tile([P, 2, ROPED_HEADS, HALF], F32)
+            for h0, acc in ((0, acc_q0), (BANK_HEADS, acc_q1)):
+                rope_products(
+                    acc[:], BANK_HEADS, cos_raw[:, t, :], sin_q[:, t, :, :],
+                    out_sb[:, h0 : h0 + BANK_HEADS, j, :], cross[:, :, h0 : h0 + BANK_HEADS, :],
+                )
+            rope_products(
+                acc_kv[:, 0 : KV_HEADS * HD], KV_HEADS, cos_k[:, t, :], sin_k[:, t, :, :],
+                out_sb[:, Q_HEADS:ROPED_HEADS, j, :], cross[:, :, Q_HEADS:ROPED_HEADS, :],
+            )
+            nc.scalar.copy(
+                out=out_sb[:, ROPED_HEADS:HEADS, j, :],
+                in_=acc_kv[:, KV_HEADS * HD :].rearrange("p (h d) -> p h d", d=HD),
+            )
+            roped = out_sb[:, 0:ROPED_HEADS, j, :].rearrange("p h (i e) -> p h i e", e=2)
+            nc.gpsimd.tensor_tensor(
+                out=roped, in0=roped, in1=cross[:].rearrange("p e h i -> p h i e"), op=ALU.add
+            )
+            if j == CHUNK - 1:
+                toks = slice(t0, t0 + CHUNK)
+                nc.sync.dma_start(out=q_view[b, :, :, toks, :], in_=out_sb[:, 0:Q_HEADS, :, :])
+                nc.sync.dma_start(
+                    out=k_view[b, :, :, toks, :], in_=out_sb[:, Q_HEADS:ROPED_HEADS, :, :]
+                )
+                nc.sync.dma_start(out=v_view[b, :, :, toks, :], in_=out_sb[:, ROPED_HEADS:HEADS, :, :])
+
+        statistics(0)
+        for step in range(TILES + 2):
+            if step % CHUNK == 0:
+                ahead = step // CHUNK + 1
+                if ahead < CHUNKS:
+                    if ahead >= 4:
+                        load_x(ahead)
+                    statistics(ahead)
+            if step < TILES:
+                normalise_and_transpose(step)
+            if 1 <= step <= TILES:
+                quantise_and_multiply(step - 1)
+            if step >= 2:
+                rope_and_store(step - 2)

@@ -57,8 +57,10 @@ def tile_block_pa_t_kernel(
         out_pool = ctx.enter_context(tc.tile_pool(name="out_pool", bufs=3))
         xt_psum = ctx.enter_context(tc.psum_pool(name="xt_psum", bufs=2))
         acc_psum = ctx.enter_context(tc.psum_pool(name="acc_psum", bufs=2))
+        gain_psum = ctx.enter_context(tc.psum_pool(name="gain_psum", bufs=1))
 
         x_tiles = {}
+        sum_sq_tiles = {}
         rstd_tiles = {}
         grouped_tiles = {}
         acc_tiles = {}
@@ -71,8 +73,8 @@ def tile_block_pa_t_kernel(
             x_tiles[chunk] = x_sb
 
         load_x(0)
-        gain = const.tile([P, D], BF16)
-        nc.scalar.dma_start(out=gain[:], in_=norm1_w.partition_broadcast(P))
+        gain_sb = const.tile([P, D], BF16)
+        nc.scalar.dma_start(out=gain_sb[:], in_=norm1_w.partition_broadcast(P))
         w_raw = const.tile([P, K_BLOCKS, N_OUT], BF16)
         w_rows = wqkv.rearrange("(kb p) n -> p kb n", p=P)
         for c in range(PASSES):
@@ -91,6 +93,12 @@ def tile_block_pa_t_kernel(
         nc.scalar.activation(out=warm[:], in_=eps[:], func=ACT.Sqrt)
         ident = const.tile([P, P], BF16)
         make_identity(nc, ident[:])
+        gain = gain_psum.tile([P, D], BF16)
+        for n0 in range(0, D, BANK):
+            nc.tensor.matmul(
+                out=gain[:, n0 : n0 + BANK], lhsT=ident[:], rhs=gain_sb[:, n0 : n0 + BANK],
+                start=True, stop=True,
+            )
 
         sin_pairs = sin_raw[:].rearrange("p t (i e) -> p t e i", e=2)
         sin_q = const.tile([P, TOK, 2, HALF], F32)
@@ -129,20 +137,25 @@ def tile_block_pa_t_kernel(
                     in_=w_grouped[:, c, n0:n1, :].rearrange("p n j -> p (n j)"),
                 )
 
-        def statistics(chunk):
-            x_sb = x_tiles[chunk]
-            sum_sq = stat.tile([P, CHUNK], F32)
-            for j in range(CHUNK):
-                squares = work.tile([P, D], BF16)
+        def sum_of_squares(n):
+            chunk, j = divmod(n, CHUNK)
+            if j == 0:
+                sum_sq = stat.tile([P, CHUNK], F32)
+                sum_sq_tiles[chunk] = sum_sq
+            sum_sq = sum_sq_tiles[chunk]
+            squares = work.tile([P, D], BF16)
+            nc.scalar.activation(
+                out=squares[:], in_=x_tiles[chunk][:, j, :], func=ACT.Square,
+                accum_out=sum_sq[:, j : j + 1],
+            )
+            if j == CHUNK - 1:
+                rms = stat.tile([P, CHUNK], F32)
                 nc.scalar.activation(
-                    out=squares[:], in_=x_sb[:, j, :], func=ACT.Square,
-                    accum_out=sum_sq[:, j : j + 1],
+                    out=rms[:], in_=sum_sq[:], func=ACT.Sqrt, bias=eps[:], scale=1.0 / D
                 )
-            rms = stat.tile([P, CHUNK], F32)
-            nc.scalar.activation(out=rms[:], in_=sum_sq[:], func=ACT.Sqrt, bias=eps[:], scale=1.0 / D)
-            rstd = stat.tile([P, CHUNK], F32)
-            nc.vector.reciprocal(out=rstd[:], in_=rms[:])
-            rstd_tiles[chunk] = rstd
+                rstd = stat.tile([P, CHUNK], F32)
+                nc.vector.reciprocal(out=rstd[:], in_=rms[:])
+                rstd_tiles[chunk] = rstd
 
         def normalise_and_transpose(n):
             chunk, j = divmod(n, CHUNK)
@@ -168,7 +181,7 @@ def tile_block_pa_t_kernel(
             )
             acc_q0 = acc_psum.tile([P, BANK], F32)
             acc_q1 = acc_psum.tile([P, BANK], F32)
-            acc_kv = acc_psum.tile([P, 2 * KV_HEADS * HD], F32)
+            acc_kv = acc_psum.tile([P, 2 * KV_HEADS * HD], F32, bufs=1)
             n0 = 0
             for acc in (acc_q0, acc_q1, acc_kv):
                 width = acc.shape[1]
@@ -185,21 +198,27 @@ def tile_block_pa_t_kernel(
                 n0 += width
             acc_tiles[n] = (acc_q0, acc_q1, acc_kv)
 
-        def rope_products(u, heads, cos_row, sin_rows, straight, cross):
+        def rope(u, heads, cos_row, sin_rows, roped):
             nc.vector.tensor_tensor(
-                out=straight,
+                out=roped,
                 in0=u.rearrange("p (h d) -> p h d", d=HD),
                 in1=cos_row.unsqueeze(1).to_broadcast([P, heads, HD]),
                 op=ALU.mult,
             )
+            cross = work.tile([P, 2, BANK_HEADS, HALF], F32, bufs=6)
             pairs = u.rearrange("p (h i e) -> p h i e", i=HALF, e=2)
             for e in range(2):
                 nc.vector.tensor_tensor(
-                    out=cross[:, e, :, :],
+                    out=cross[:, e, 0:heads, :],
                     in0=pairs[:, :, :, 1 - e],
                     in1=sin_rows[:, e, :].unsqueeze(1).to_broadcast([P, heads, HALF]),
                     op=ALU.mult,
                 )
+            by_pair = roped.rearrange("p h (i e) -> p h i e", e=2)
+            nc.gpsimd.tensor_tensor(
+                out=by_pair, in0=by_pair,
+                in1=cross[:, :, 0:heads, :].rearrange("p e h i -> p h i e"), op=ALU.add,
+            )
 
         def rope_and_store(n):
             chunk, j = divmod(n, CHUNK)
@@ -210,24 +229,19 @@ def tile_block_pa_t_kernel(
                 out_tiles[chunk] = out_sb
             out_sb = out_tiles[chunk]
             acc_q0, acc_q1, acc_kv = acc_tiles.pop(n)
-            cross = work.tile([P, 2, ROPED_HEADS, HALF], F32)
-            for h0, acc in ((0, acc_q0), (BANK_HEADS, acc_q1)):
-                rope_products(
-                    acc[:], BANK_HEADS, cos_raw[:, t, :], sin_q[:, t, :, :],
-                    out_sb[:, h0 : h0 + BANK_HEADS, j, :], cross[:, :, h0 : h0 + BANK_HEADS, :],
-                )
-            rope_products(
+            rope(
                 acc_kv[:, 0 : KV_HEADS * HD], KV_HEADS, cos_k[:, t, :], sin_k[:, t, :, :],
-                out_sb[:, Q_HEADS:ROPED_HEADS, j, :], cross[:, :, Q_HEADS:ROPED_HEADS, :],
+                out_sb[:, Q_HEADS:ROPED_HEADS, j, :],
             )
             nc.scalar.copy(
                 out=out_sb[:, ROPED_HEADS:HEADS, j, :],
                 in_=acc_kv[:, KV_HEADS * HD :].rearrange("p (h d) -> p h d", d=HD),
             )
-            roped = out_sb[:, 0:ROPED_HEADS, j, :].rearrange("p h (i e) -> p h i e", e=2)
-            nc.gpsimd.tensor_tensor(
-                out=roped, in0=roped, in1=cross[:].rearrange("p e h i -> p h i e"), op=ALU.add
-            )
+            for h0, acc in ((0, acc_q0), (BANK_HEADS, acc_q1)):
+                rope(
+                    acc[:], BANK_HEADS, cos_raw[:, t, :], sin_q[:, t, :, :],
+                    out_sb[:, h0 : h0 + BANK_HEADS, j, :],
+                )
             if j == CHUNK - 1:
                 toks = slice(t0, t0 + CHUNK)
                 nc.sync.dma_start(out=q_view[b, :, :, toks, :], in_=out_sb[:, 0:Q_HEADS, :, :])
@@ -236,14 +250,13 @@ def tile_block_pa_t_kernel(
                 )
                 nc.sync.dma_start(out=v_view[b, :, :, toks, :], in_=out_sb[:, ROPED_HEADS:HEADS, :, :])
 
-        statistics(0)
+        for n in range(CHUNK):
+            sum_of_squares(n)
         for step in range(TILES + 2):
-            if step % CHUNK == 0:
-                ahead = step // CHUNK + 1
-                if ahead < CHUNKS:
-                    if ahead >= 4:
-                        load_x(ahead)
-                    statistics(ahead)
+            if step % CHUNK == 0 and 4 <= step // CHUNK + 3 < CHUNKS:
+                load_x(step // CHUNK + 3)
+            if step + CHUNK < TILES:
+                sum_of_squares(step + CHUNK)
             if step < TILES:
                 normalise_and_transpose(step)
             if 1 <= step <= TILES:

@@ -250,16 +250,17 @@ def tile_block_pa_t_kernel(
                 )
                 nc.sync.dma_start(out=v_view[b, :, :, toks, :], in_=out_sb[:, ROPED_HEADS:HEADS, :, :])
 
-        for n in range(CHUNK):
-            sum_of_squares(n)
-        for step in range(TILES + 2):
-            if step % CHUNK == 0 and 4 <= step // CHUNK + 3 < CHUNKS:
-                load_x(step // CHUNK + 3)
-            if step + CHUNK < TILES:
-                sum_of_squares(step + CHUNK)
-            if step < TILES:
-                normalise_and_transpose(step)
-            if 1 <= step <= TILES:
-                quantise_and_multiply(step - 1)
-            if step >= 2:
-                rope_and_store(step - 2)
+        with tc.manual_schedule():
+            for n in range(CHUNK):
+                sum_of_squares(n)
+            for step in range(TILES + 2):
+                if step % CHUNK == 0 and 4 <= step // CHUNK + 3 < CHUNKS:
+                    load_x(step // CHUNK + 3)
+                if step + CHUNK < TILES:
+                    sum_of_squares(step + CHUNK)
+                if step < TILES:
+                    normalise_and_transpose(step)
+                if 1 <= step <= TILES:
+                    quantise_and_multiply(step - 1)
+                if step >= 2:
+                    rope_and_store(step - 2)

@@ -57,10 +57,8 @@ def tile_block_pa_t_kernel(
         out_pool = ctx.enter_context(tc.tile_pool(name="out_pool", bufs=3))
         xt_psum = ctx.enter_context(tc.psum_pool(name="xt_psum", bufs=2))
         acc_psum = ctx.enter_context(tc.psum_pool(name="acc_psum", bufs=2))
-        gain_psum = ctx.enter_context(tc.psum_pool(name="gain_psum", bufs=1))
 
         x_tiles = {}
-        sum_sq_tiles = {}
         rstd_tiles = {}
         grouped_tiles = {}
         acc_tiles = {}
@@ -73,8 +71,8 @@ def tile_block_pa_t_kernel(
             x_tiles[chunk] = x_sb
 
         load_x(0)
-        gain_sb = const.tile([P, D], BF16)
-        nc.scalar.dma_start(out=gain_sb[:], in_=norm1_w.partition_broadcast(P))
+        gain = const.tile([P, D], BF16)
+        nc.scalar.dma_start(out=gain[:], in_=norm1_w.partition_broadcast(P))
         w_raw = const.tile([P, K_BLOCKS, N_OUT], BF16)
         w_rows = wqkv.rearrange("(kb p) n -> p kb n", p=P)
         for c in range(PASSES):
@@ -93,12 +91,6 @@ def tile_block_pa_t_kernel(
         nc.scalar.activation(out=warm[:], in_=eps[:], func=ACT.Sqrt)
         ident = const.tile([P, P], BF16)
         make_identity(nc, ident[:])
-        gain = gain_psum.tile([P, D], BF16)
-        for n0 in range(0, D, BANK):
-            nc.tensor.matmul(
-                out=gain[:, n0 : n0 + BANK], lhsT=ident[:], rhs=gain_sb[:, n0 : n0 + BANK],
-                start=True, stop=True,
-            )
 
         sin_pairs = sin_raw[:].rearrange("p t (i e) -> p t e i", e=2)
         sin_q = const.tile([P, TOK, 2, HALF], F32)
@@ -137,25 +129,20 @@ def tile_block_pa_t_kernel(
                     in_=w_grouped[:, c, n0:n1, :].rearrange("p n j -> p (n j)"),
                 )
 
-        def sum_of_squares(n):
-            chunk, j = divmod(n, CHUNK)
-            if j == 0:
-                sum_sq = stat.tile([P, CHUNK], F32)
-                sum_sq_tiles[chunk] = sum_sq
-            sum_sq = sum_sq_tiles[chunk]
-            squares = work.tile([P, D], BF16)
-            nc.scalar.activation(
-                out=squares[:], in_=x_tiles[chunk][:, j, :], func=ACT.Square,
-                accum_out=sum_sq[:, j : j + 1],
-            )
-            if j == CHUNK - 1:
-                rms = stat.tile([P, CHUNK], F32)
+        def statistics(chunk):
+            x_sb = x_tiles[chunk]
+            sum_sq = stat.tile([P, CHUNK], F32)
+            for j in range(CHUNK):
+                squares = work.tile([P, D], BF16)
                 nc.scalar.activation(
-                    out=rms[:], in_=sum_sq[:], func=ACT.Sqrt, bias=eps[:], scale=1.0 / D
+                    out=squares[:], in_=x_sb[:, j, :], func=ACT.Square,
+                    accum_out=sum_sq[:, j : j + 1],
                 )
-                rstd = stat.tile([P, CHUNK], F32)
-                nc.vector.reciprocal(out=rstd[:], in_=rms[:])
-                rstd_tiles[chunk] = rstd
+            rms = stat.tile([P, CHUNK], F32)
+            nc.scalar.activation(out=rms[:], in_=sum_sq[:], func=ACT.Sqrt, bias=eps[:], scale=1.0 / D)
+            rstd = stat.tile([P, CHUNK], F32)
+            nc.vector.reciprocal(out=rstd[:], in_=rms[:])
+            rstd_tiles[chunk] = rstd
 
         def normalise_and_transpose(n):
             chunk, j = divmod(n, CHUNK)
@@ -181,7 +168,7 @@ def tile_block_pa_t_kernel(
             )
             acc_q0 = acc_psum.tile([P, BANK], F32)
             acc_q1 = acc_psum.tile([P, BANK], F32)
-            acc_kv = acc_psum.tile([P, 2 * KV_HEADS * HD], F32, bufs=1)
+            acc_kv = acc_psum.tile([P, 2 * KV_HEADS * HD], F32)
             n0 = 0
             for acc in (acc_q0, acc_q1, acc_kv):
                 width = acc.shape[1]
@@ -198,26 +185,19 @@ def tile_block_pa_t_kernel(
                 n0 += width
             acc_tiles[n] = (acc_q0, acc_q1, acc_kv)
 
-        def rope(u, heads, cos_row, sin_rows, roped):
+        def rope_products(u, heads, cos_row, sin_rows, straight, cross):
             nc.vector.tensor_tensor(
-                out=roped,
+                out=straight,
                 in0=u.rearrange("p (h d) -> p h d", d=HD),
                 in1=cos_row.unsqueeze(1).to_broadcast([P, heads, HD]),
                 op=ALU.mult,
             )
-            cross = work.tile([P, 2, BANK_HEADS, HALF], F32, bufs=6)
-            pairs = u.rearrange("p (h i e) -> p h i e", i=HALF, e=2)
-            for e in range(2):
-                nc.vector.tensor_tensor(
-                    out=cross[:, e, 0:heads, :],
-                    in0=pairs[:, :, :, 1 - e],
-                    in1=sin_rows[:, e, :].unsqueeze(1).to_broadcast([P, heads, HALF]),
-                    op=ALU.mult,
-                )
-            by_pair = roped.rearrange("p h (i e) -> p h i e", e=2)
-            nc.gpsimd.tensor_tensor(
-                out=by_pair, in0=by_pair,
-                in1=cross[:, :, 0:heads, :].rearrange("p e h i -> p h i e"), op=ALU.add,
+            partners = u.rearrange("p (h i e) -> p e h i", i=HALF, e=2)[:, ::-1, :, :]
+            nc.vector.tensor_tensor(
+                out=cross,
+                in0=partners,
+                in1=sin_rows.unsqueeze(2).to_broadcast([P, 2, heads, HALF]),
+                op=ALU.mult,
             )
 
         def rope_and_store(n):
@@ -229,19 +209,24 @@ def tile_block_pa_t_kernel(
                 out_tiles[chunk] = out_sb
             out_sb = out_tiles[chunk]
             acc_q0, acc_q1, acc_kv = acc_tiles.pop(n)
-            rope(
+            cross = work.tile([P, 2, ROPED_HEADS, HALF], F32)
+            for h0, acc in ((0, acc_q0), (BANK_HEADS, acc_q1)):
+                rope_products(
+                    acc[:], BANK_HEADS, cos_raw[:, t, :], sin_q[:, t, :, :],
+                    out_sb[:, h0 : h0 + BANK_HEADS, j, :], cross[:, :, h0 : h0 + BANK_HEADS, :],
+                )
+            rope_products(
                 acc_kv[:, 0 : KV_HEADS * HD], KV_HEADS, cos_k[:, t, :], sin_k[:, t, :, :],
-                out_sb[:, Q_HEADS:ROPED_HEADS, j, :],
+                out_sb[:, Q_HEADS:ROPED_HEADS, j, :], cross[:, :, Q_HEADS:ROPED_HEADS, :],
             )
             nc.scalar.copy(
                 out=out_sb[:, ROPED_HEADS:HEADS, j, :],
                 in_=acc_kv[:, KV_HEADS * HD :].rearrange("p (h d) -> p h d", d=HD),
             )
-            for h0, acc in ((0, acc_q0), (BANK_HEADS, acc_q1)):
-                rope(
-                    acc[:], BANK_HEADS, cos_raw[:, t, :], sin_q[:, t, :, :],
-                    out_sb[:, h0 : h0 + BANK_HEADS, j, :],
-                )
+            roped = out_sb[:, 0:ROPED_HEADS, j, :].rearrange("p h (i e) -> p h i e", e=2)
+            nc.gpsimd.tensor_tensor(
+                out=roped, in0=roped, in1=cross[:].rearrange("p e h i -> p h i e"), op=ALU.add
+            )
             if j == CHUNK - 1:
                 toks = slice(t0, t0 + CHUNK)
                 nc.sync.dma_start(out=q_view[b, :, :, toks, :], in_=out_sb[:, 0:Q_HEADS, :, :])
@@ -250,17 +235,17 @@ def tile_block_pa_t_kernel(
                 )
                 nc.sync.dma_start(out=v_view[b, :, :, toks, :], in_=out_sb[:, ROPED_HEADS:HEADS, :, :])
 
-        with tc.manual_schedule():
-            for n in range(CHUNK):
-                sum_of_squares(n)
-            for step in range(TILES + 2):
-                if step % CHUNK == 0 and 4 <= step // CHUNK + 3 < CHUNKS:
-                    load_x(step // CHUNK + 3)
-                if step + CHUNK < TILES:
-                    sum_of_squares(step + CHUNK)
-                if step < TILES:
-                    normalise_and_transpose(step)
-                if 1 <= step <= TILES:
-                    quantise_and_multiply(step - 1)
-                if step >= 2:
-                    rope_and_store(step - 2)
+        statistics(0)
+        for step in range(TILES + 2):
+            if step % CHUNK == 0:
+                ahead = step // CHUNK + 1
+                if ahead < CHUNKS:
+                    if ahead >= 4:
+                        load_x(ahead)
+                    statistics(ahead)
+            if step < TILES:
+                normalise_and_transpose(step)
+            if 1 <= step <= TILES:
+                quantise_and_multiply(step - 1)
+            if step >= 2:
+                rope_and_store(step - 2)

from contextlib import ExitStack

import concourse.mybir as mybir
from concourse.masks import make_identity

F32 = mybir.dt.float32
BF16 = mybir.dt.bfloat16
U32 = mybir.dt.uint32
U8 = mybir.dt.uint8
FP8X4 = mybir.dt.float8_e4m3fn_x4
ALU = mybir.AluOpType
ACT = mybir.ActivationFunctionType

P = 128
BATCH = 2
SEQ = 2048
D = 1024
HD = 64
HALF = HD // 2
Q_HEADS = 16
KV_HEADS = 2
ROPED_HEADS = Q_HEADS + KV_HEADS
HEADS = Q_HEADS + 2 * KV_HEADS
N_OUT = HEADS * HD
EPS = 1e-5

PACK = 4
K_PASS = P * PACK
PASSES = D // K_PASS
K_BLOCKS = D // P

TOK = SEQ // P
CHUNK = 4
TILES = BATCH * TOK
CHUNKS = TILES // CHUNK
BANK = 512
BANK_HEADS = BANK // HD

FLOPS = 2 * BATCH * SEQ * D * N_OUT


def tile_block_pa_t_kernel(
    tc, x, norm1_w, wqkv, rope_sin, rope_cos, out_0, out_1, out_2
):
    nc = tc.nc

    x_view = x.rearrange("b (p t) k -> b p t k", t=TOK)
    q_view = out_0.rearrange("b r g (p t) d -> b p (r g) t d", t=TOK)
    k_view = out_1.rearrange("b g (p t) d -> b p g t d", t=TOK)
    v_view = out_2.rearrange("b g (p t) d -> b p g t d", t=TOK)

    with ExitStack() as ctx:
        const = ctx.enter_context(tc.tile_pool(name="const", bufs=1))
        x_pool = ctx.enter_context(tc.tile_pool(name="x_pool", bufs=4))
        stat = ctx.enter_context(tc.tile_pool(name="stat", bufs=3))
        work = ctx.enter_context(tc.tile_pool(name="work", bufs=3))
        out_pool = ctx.enter_context(tc.tile_pool(name="out_pool", bufs=3))
        xt_psum = ctx.enter_context(tc.psum_pool(name="xt_psum", bufs=2))
        acc_psum = ctx.enter_context(tc.psum_pool(name="acc_psum", bufs=2))

        x_tiles = {}
        rstd_tiles = {}
        grouped_tiles = {}
        acc_tiles = {}
        out_tiles = {}

        def load_x(chunk):
            b, t0 = divmod(chunk * CHUNK, TOK)
            x_sb = x_pool.tile([P, CHUNK, D], BF16)
            nc.sync.dma_start(out=x_sb[:], in_=x_view[b, :, t0 : t0 + CHUNK, :])
            x_tiles[chunk] = x_sb

        load_x(0)
        gain = const.tile([P, D], BF16)
        nc.scalar.dma_start(out=gain[:], in_=norm1_w.partition_broadcast(P))
        w_raw = const.tile([P, K_BLOCKS, N_OUT], BF16)
        w_rows = wqkv.rearrange("(kb p) n -> p kb n", p=P)
        for c in range(PASSES):
            slots = slice(c * PACK, (c + 1) * PACK)
            nc.sync.dma_start(out=w_raw[:, slots, :], in_=w_rows[:, slots, :])
        cos_raw = const.tile([P, TOK, HD], BF16)
        nc.sync.dma_start(out=cos_raw[:], in_=rope_cos.rearrange("(p t) d -> p t d", t=TOK))
        sin_raw = const.tile([P, TOK, HD], BF16)
        nc.sync.dma_start(out=sin_raw[:], in_=rope_sin.rearrange("(p t) d -> p t d", t=TOK))
        for chunk in range(1, 4):
            load_x(chunk)

        eps = const.tile([P, 1], F32)
        nc.vector.memset(eps[:], EPS)
        warm = const.tile([P, 1], F32)
        nc.scalar.activation(out=warm[:], in_=eps[:], func=ACT.Sqrt)
        ident = const.tile([P, P], BF16)
        make_identity(nc, ident[:])

        sin_pairs = sin_raw[:].rearrange("p t (i e) -> p t e i", e=2)
        sin_q = const.tile([P, TOK, 2, HALF], F32)
        sin_k = const.tile([P, TOK, 2, HALF], F32)
        cos_k = const.tile([P, TOK, HD], F32)
        k_scale = HD**-0.5
        for table, scale in ((sin_q, 1.0), (sin_k, k_scale)):
            for e, sign in ((0, -1.0), (1, 1.0)):
                nc.gpsimd.tensor_scalar(
                    out=table[:, :, e, :],
                    in0=sin_pairs[:, :, e, :],
                    scalar1=sign * scale,
                    scalar2=0.0,
                    op0=ALU.mult,
                    op1=ALU.add,
                )
        nc.gpsimd.tensor_scalar(
            out=cos_k[:], in0=cos_raw[:], scalar1=k_scale, scalar2=0.0, op0=ALU.mult, op1=ALU.add
        )

        w_grouped = const.tile([P, PASSES, N_OUT, PACK], BF16, align_bytes=64)
        w_codes = const.tile([P, PASSES, N_OUT], U32, align_bytes=64)
        w_scales = const.tile([P, PASSES, N_OUT], U8, align_bytes=64)
        for c in range(PASSES):
            src = w_raw[:, c * PACK : (c + 1) * PACK, :].rearrange("p j (m i) -> p m j i", i=4)
            dst = w_grouped[:, c, :, :].rearrange("p (m i) j -> p m j i", i=4)
            if c == 0:
                nc.vector.tensor_copy(out=dst, in_=src)
            else:
                nc.scalar.copy(out=dst, in_=src)
        for c in range(PASSES):
            for n0, n1 in ((0, 1024), (1024, N_OUT)):
                nc.vector.quantize_mx(
                    out=w_codes[:, c, n0:n1].bitcast(FP8X4),
                    scales=w_scales[:, c, n0:n1],
                    in_=w_grouped[:, c, n0:n1, :].rearrange("p n j -> p (n j)"),
                )

        def statistics(chunk):
            x_sb = x_tiles[chunk]
            sum_sq = stat.tile([P, CHUNK], F32)
            for j in range(CHUNK):
                squares = work.tile([P, D], BF16)
                nc.scalar.activation(
                    out=squares[:], in_=x_sb[:, j, :], func=ACT.Square,
                    accum_out=sum_sq[:, j : j + 1],
                )
            rms = stat.tile([P, CHUNK], F32)
            nc.scalar.activation(out=rms[:], in_=sum_sq[:], func=ACT.Sqrt, bias=eps[:], scale=1.0 / D)
            rstd = stat.tile([P, CHUNK], F32)
            nc.vector.reciprocal(out=rstd[:], in_=rms[:])
            rstd_tiles[chunk] = rstd

        def normalise_and_transpose(n):
            chunk, j = divmod(n, CHUNK)
            xn = work.tile([P, D], BF16)
            nc.vector.scalar_tensor_tensor(
                out=xn[:], in0=x_tiles[chunk][:, j, :], scalar=rstd_tiles[chunk][:, j : j + 1],
                in1=gain[:], op0=ALU.mult, op1=ALU.mult,
            )
            xt = xt_psum.tile([P, K_BLOCKS, P], BF16)
            for kb in range(K_BLOCKS):
                nc.tensor.transpose(xt[:, kb, :], xn[:, kb * P : (kb + 1) * P], ident[:])
            grouped = work.tile([P, PASSES, P, PACK], BF16, align_bytes=64)
            nc.scalar.copy(out=grouped[:], in_=xt[:].rearrange("p (c j) r -> p c r j", j=PACK))
            grouped_tiles[n] = grouped

        def quantise_and_multiply(n):
            codes = work.tile([P, PASSES, P], U32, align_bytes=64)
            scales = work.tile([P, PASSES, P], U8, align_bytes=64)
            nc.vector.quantize_mx(
                out=codes[:].rearrange("p c r -> p (c r)").bitcast(FP8X4),
                scales=scales[:].rearrange("p c r -> p (c r)"),
                in_=grouped_tiles.pop(n)[:].rearrange("p c r j -> p (c r j)"),
            )
            acc_q0 = acc_psum.tile([P, BANK], F32)
            acc_q1 = acc_psum.tile([P, BANK], F32)
            acc_kv = acc_psum.tile([P, 2 * KV_HEADS * HD], F32)
            n0 = 0
            for acc in (acc_q0, acc_q1, acc_kv):
                width = acc.shape[1]
                for c in range(PASSES):
                    nc.tensor.matmul_mx(
                        out=acc[:],
                        lhsT=codes[:, c, :].bitcast(FP8X4),
                        lhsT_scale=scales[:, c, :],
                        rhs=w_codes[:, c, n0 : n0 + width].bitcast(FP8X4),
                        rhs_scale=w_scales[:, c, n0 : n0 + width],
                        start=(c == 0),
                        stop=(c == PASSES - 1),
                    )
                n0 += width
            acc_tiles[n] = (acc_q0, acc_q1, acc_kv)

        def rope_products(u, heads, cos_row, sin_rows, straight, cross):
            nc.vector.tensor_tensor(
                out=straight,
                in0=u.rearrange("p (h d) -> p h d", d=HD),
                in1=cos_row.unsqueeze(1).to_broadcast([P, heads, HD]),
                op=ALU.mult,
            )
            partners = u.rearrange("p (h i e) -> p e h i", i=HALF, e=2)[:, ::-1, :, :]
            nc.vector.tensor_tensor(
                out=cross,
                in0=partners,
                in1=sin_rows.unsqueeze(2).to_broadcast([P, 2, heads, HALF]),
                op=ALU.mult,
            )

        def rope_and_store(n):
            chunk, j = divmod(n, CHUNK)
            b, t0 = divmod(chunk * CHUNK, TOK)
            t = t0 + j
            if j == 0:
                out_sb = out_pool.tile([P, HEADS, CHUNK, HD], F32)
                out_tiles[chunk] = out_sb
            out_sb = out_tiles[chunk]
            acc_q0, acc_q1, acc_kv = acc_tiles.pop(n)
            cross = work.tile([P, 2, ROPED_HEADS, HALF], F32)
            for h0, acc in ((0, acc_q0), (BANK_HEADS, acc_q1)):
                rope_products(
                    acc[:], BANK_HEADS, cos_raw[:, t, :], sin_q[:, t, :, :],
                    out_sb[:, h0 : h0 + BANK_HEADS, j, :], cross[:, :, h0 : h0 + BANK_HEADS, :],
                )
            rope_products(
                acc_kv[:, 0 : KV_HEADS * HD], KV_HEADS, cos_k[:, t, :], sin_k[:, t, :, :],
                out_sb[:, Q_HEADS:ROPED_HEADS, j, :], cross[:, :, Q_HEADS:ROPED_HEADS, :],
            )
            nc.scalar.copy(
                out=out_sb[:, ROPED_HEADS:HEADS, j, :],
                in_=acc_kv[:, KV_HEADS * HD :].rearrange("p (h d) -> p h d", d=HD),
            )
            roped = out_sb[:, 0:ROPED_HEADS, j, :].rearrange("p h (i e) -> p h i e", e=2)
            nc.gpsimd.tensor_tensor(
                out=roped, in0=roped, in1=cross[:].rearrange("p e h i -> p h i e"), op=ALU.add
            )
            if j == CHUNK - 1:
                toks = slice(t0, t0 + CHUNK)
                nc.sync.dma_start(out=q_view[b, :, :, toks, :], in_=out_sb[:, 0:Q_HEADS, :, :])
                nc.sync.dma_start(
                    out=k_view[b, :, :, toks, :], in_=out_sb[:, Q_HEADS:ROPED_HEADS, :, :]
                )
                nc.sync.dma_start(out=v_view[b, :, :, toks, :], in_=out_sb[:, ROPED_HEADS:HEADS, :, :])

        statistics(0)
        for step in range(TILES + 2):
            if step % CHUNK == 0:
                ahead = step // CHUNK + 1
                if ahead < CHUNKS:
                    if ahead >= 4:
                        load_x(ahead)
                    statistics(ahead)
            if step < TILES:
                normalise_and_transpose(step)
            if 1 <= step <= TILES:
                quantise_and_multiply(step - 1)
            if step >= 2:
                rope_and_store(step - 2)
